import numpy as np
import ml_dtypes


def mxq(x, axis, fmt="e4m3"):
    dtype, down = {"e4m3": (ml_dtypes.float8_e4m3fn, 7), "e5m2": (ml_dtypes.float8_e5m2, 14)}[fmt]
    v = np.moveaxis(np.asarray(x, np.float32).astype(ml_dtypes.bfloat16).astype(np.float64), axis, -1)
    blocks = v.reshape(v.shape[:-1] + (-1, 32))
    amax = np.abs(blocks).max(-1, keepdims=True)
    byte = np.maximum(np.where(amax > 0, np.frexp(amax)[1] - 1 + 127, 0) - down, 1)
    scale = np.exp2(byte - 127.0)
    codes = (blocks / scale).astype(np.float32).astype(dtype).astype(np.float64)
    return np.moveaxis((codes * scale).reshape(v.shape), -1, axis)


WIDE = False


def mx_kscale(k):
    if not WIDE:
        return np.ones(k)
    levels = np.array([10, -10, 5, -5, 0])
    a = np.random.permutation(np.resize(levels, k // 512 * 4)).reshape(k // 512, 4)
    idx = np.arange(k)
    return np.exp2(a[idx // 512, idx % 128 // 32])


BF16 = ml_dtypes.bfloat16


def bf(x):
    return np.asarray(x, np.float32).astype(BF16)


def f64(x):
    return np.asarray(x).astype(np.float64)


E2M1 = np.array([0.0, 0.5, 1.0, 1.5, 2.0, 3.0, 4.0, 6.0, -0.0, -0.5, -1.0, -1.5, -2.0, -3.0, -4.0, -6.0])


def pack_weight(w, fmt):
    k, n = w.shape
    w = f64(bf(w)).reshape(k // 32, 32, n)
    amax = np.abs(w).max(1)
    if fmt == "e4m3":
        byte = np.frexp(amax)[1] - 1 + 127 - 7
    else:
        mant, ex = np.frexp(amax / 6.0)
        byte = np.where(mant > 0.5, ex, ex - 1) + 127
    byte = np.clip(np.where(amax > 0, byte, 1), 1, 254)
    scaled = (w * np.exp2(127.0 - byte)[:, None, :]).reshape(k, n).astype(np.float32)
    by_word = np.ascontiguousarray(scaled.reshape(k // 512, 128, 4, n).transpose(0, 1, 3, 2))
    if fmt == "e4m3":
        words = by_word.astype(ml_dtypes.float8_e4m3fn).view(np.uint8)
    else:
        c = by_word.astype(ml_dtypes.float4_e2m1fn).view(np.uint8) & 0xF
        words = c[..., 0::2] | (c[..., 1::2] << 4)
    return np.ascontiguousarray(words), np.ascontiguousarray(byte.astype(np.uint8).reshape(k // 512, 16, n))


def unpack_weight(words, scales, fmt):
    g, p, n, _ = words.shape
    if fmt == "e4m3":
        vals = np.ascontiguousarray(words).view(ml_dtypes.float8_e4m3fn).astype(np.float64)
    else:
        nib = np.empty((g, p, n, 4), np.uint8)
        nib[..., 0::2] = words & 0xF
        nib[..., 1::2] = words >> 4
        vals = E2M1[nib]
    vals = vals * np.repeat(np.exp2(scales.astype(np.float64) - 127.0), 8, axis=1)[..., None]
    return vals.transpose(0, 1, 3, 2).reshape(g * 512, n)

def pack4(w):
    words, scales = pack_weight(w, "e2m1")
    return words.reshape(words.shape[0], 128, -1), scales


def unpack4(words, scales):
    return unpack_weight(words.reshape(words.shape[0], 128, -1, 2), scales, "e2m1")


B, S, E, N_HEAD, MP_NUM, ROTARY_DIM = 2, 128, 2048, 16, 4, 64
HEAD_DIM = E // N_HEAD
LOCAL = E // MP_NUM
ROPE_BASE = 10000.0


def rotate_every_two(x):
    x1 = x[..., 0::2]
    x2 = x[..., 1::2]
    return np.stack((-x2, x1), axis=-1).reshape(x.shape)


def rope(x, sin, cos):
    x_rot = x[..., :ROTARY_DIM]
    x_pass = x[..., ROTARY_DIM:]
    x_rot = x_rot * cos + rotate_every_two(x_rot) * sin
    return np.concatenate([x_rot, x_pass], axis=-1)


def setup_inputs():
    s = mx_kscale(E)
    hidden_states = bf(np.random.standard_normal((B, S, E)) * s)
    w = np.random.standard_normal((3 * E, E)) / np.sqrt(E) / s[None, :]
    words, scales = pack4(w.T)
    return {"hidden_states": hidden_states,
            "w_qkv_words": words,
            "w_qkv_scales": scales}


def reference(hidden_states, w_qkv_words, w_qkv_scales):
    qkv = mxq(f64(hidden_states), 2, "e4m3") @ unpack4(w_qkv_words, w_qkv_scales)
    qkv = qkv.reshape(B, S, MP_NUM, 3 * LOCAL)
    q = qkv[..., :LOCAL].reshape(B, S, N_HEAD, HEAD_DIM)
    v = qkv[..., LOCAL:2 * LOCAL].reshape(B, S, N_HEAD, HEAD_DIM)
    k = qkv[..., 2 * LOCAL:].reshape(B, S, N_HEAD, HEAD_DIM)
    inv_freq = 1.0 / (ROPE_BASE ** (np.arange(0, ROTARY_DIM, 2) / ROTARY_DIM))
    freqs = np.arange(S)[:, None] * inv_freq[None, :]
    sin = np.repeat(np.sin(freqs), 2, axis=-1)[None, :, None, :]
    cos = np.repeat(np.cos(freqs), 2, axis=-1)[None, :, None, :]
    q = rope(q, sin, cos)
    k = rope(k, sin, cos)
    return q.transpose(0, 2, 1, 3), k.transpose(0, 2, 1, 3), v.transpose(0, 2, 1, 3)

@@ -1,0 +1,210 @@
+import math
+
+import concourse.mybir as mybir
+from concourse.masks import make_identity
+
+F32 = mybir.dt.float32
+BF16 = mybir.dt.bfloat16
+I32 = mybir.dt.int32
+U32 = mybir.dt.uint32
+U8 = mybir.dt.uint8
+FP8X4 = mybir.dt.float8_e4m3fn_x4
+FP4X4 = mybir.dt.float4_e2m1fn_x4
+ALU = mybir.AluOpType
+ACT = mybir.ActivationFunctionType
+
+P = 128
+BATCH = 2
+CHANNELS = 2048
+PACK = 4
+PASSES = CHANNELS // (P * PACK)
+PARITIES = 2
+
+SHARDS = 4
+HEADS = 4
+HEAD_DIM = 128
+BLOCK = HEADS * HEAD_DIM
+SHARD_COLS = 3 * BLOCK
+SCALE_ROWS = 16
+
+ROTARY = 64
+PAIRS = ROTARY // 2
+ROPE_BASE = 10000.0
+ROUND_MAGIC = 1.5 * 2.0**23
+
+FLOPS = 2 * BATCH * 128 * CHANNELS * SHARDS * SHARD_COLS
+
+
+def load_tokens(nc, pool, hidden_states):
+    x_sb = pool.tile([P, PARITIES, CHANNELS], BF16)
+    for b in range(BATCH):
+        nc.sync.dma_start(
+            out=x_sb[b:P:BATCH],
+            in_=hidden_states[b].rearrange("(pair par) e -> pair par e", par=PARITIES),
+        )
+    return x_sb
+
+
+def load_shard(nc, pool, w_qkv_words, w_qkv_scales, s):
+    scales = pool.tile([P, PASSES, SHARD_COLS], U8, name="w_scales%d" % s, align_bytes=64)
+    scales_i32 = scales[:].bitcast(I32)
+    nc.vector.memset(scales_i32, 0)
+    cols = slice(s * SHARD_COLS // 4, (s + 1) * SHARD_COLS // 4)
+    for q in range(SCALE_ROWS // 2):
+        nc.sync.dma_start(
+            out=scales_i32[32 * (q // 4) + q % 4 : P : 64],
+            in_=w_qkv_scales.bitcast(I32)[:, q : SCALE_ROWS : SCALE_ROWS // 2, cols].rearrange("g q n -> q g n"),
+        )
+    words = pool.tile([P, PASSES, 2 * SHARD_COLS], U8, name="w_words%d" % s, align_bytes=64)
+    cols = slice(s * SHARD_COLS // 2, (s + 1) * SHARD_COLS // 2)
+    nc.sync.dma_start(
+        out=words[:].bitcast(I32),
+        in_=w_qkv_words.bitcast(I32)[:, :, cols].rearrange("g p n -> p g n"),
+    )
+    return words, scales
+
+
+def rotary_tables(nc, pool):
+    partition = pool.tile([P, 1], I32)
+    nc.gpsimd.iota(partition[:], pattern=[[0, 1]], base=0, channel_multiplier=1)
+    position = pool.tile([P, PARITIES], I32)
+    for par in range(PARITIES):
+        nc.vector.tensor_scalar(
+            out=position[:, par : par + 1],
+            in0=partition[:],
+            scalar1=P - 2,
+            scalar2=par,
+            op0=ALU.bitwise_and,
+            op1=ALU.bitwise_or,
+        )
+    phase = pool.tile([P, 3 * ROTARY], F32)
+    turns = phase[:, 0:ROTARY].rearrange("p (par i) -> p par i", par=PARITIES)
+    nc.vector.tensor_scalar(
+        out=turns[:, :, 0:1],
+        in0=position[:].unsqueeze(2),
+        scalar1=1.0 / (2.0 * math.pi),
+        scalar2=None,
+        op0=ALU.mult,
+    )
+    n = 1
+    while n < PAIRS:
+        nc.vector.tensor_scalar(
+            out=turns[:, :, n : 2 * n],
+            in0=turns[:, :, 0:n],
+            scalar1=ROPE_BASE ** (-2.0 * n / ROTARY),
+            scalar2=None,
+            op0=ALU.mult,
+        )
+        n *= 2
+    nc.vector.tensor_scalar(
+        out=phase[:, ROTARY : 3 * ROTARY].rearrange("p (par i two) -> p par i two", par=PARITIES, two=2),
+        in0=turns.unsqueeze(3).to_broadcast([P, PARITIES, PAIRS, 2]),
+        scalar1=0.25,
+        scalar2=None,
+        op0=ALU.add,
+    )
+    whole = pool.tile([P, 3 * ROTARY], F32)
+    nc.vector.tensor_scalar(
+        out=whole[:], in0=phase[:], scalar1=ROUND_MAGIC, scalar2=ROUND_MAGIC, op0=ALU.add, op1=ALU.subtract
+    )
+    nc.vector.tensor_tensor(out=phase[:], in0=phase[:], in1=whole[:], op=ALU.subtract)
+    trig = pool.tile([P, 3 * ROTARY], F32)
+    nc.scalar.activation(out=trig[:], in_=phase[:], func=ACT.Sin, scale=2.0 * math.pi)
+    minus = pool.tile([P, ROTARY], F32)
+    nc.scalar.activation(out=minus[:], in_=phase[:, 0:ROTARY], func=ACT.Sin, scale=-2.0 * math.pi)
+    cos = trig[:, ROTARY : 3 * ROTARY].rearrange("p (par c) -> p par c", par=PARITIES)
+    sin = trig[:, 0:ROTARY].rearrange("p (par i) -> p par i", par=PARITIES)
+    neg_sin = minus[:].rearrange("p (par i) -> p par i", par=PARITIES)
+    return cos, sin, neg_sin
+
+
+def quantise_tokens(nc, pool, banks, x_sb):
+    identity = pool.tile([P, P], F32)
+    make_identity(nc, identity[:])
+    x_words = x_sb[:].bitcast(F32)
+    words_a_pass = P * PACK // 2
+    grouped = pool.tile([P, PARITIES, PASSES, P, PACK], BF16, align_bytes=64)
+    grouped_words = grouped[:].bitcast(F32)
+    codes = pool.tile([P, PARITIES, PASSES, P], U32, align_bytes=64)
+    scales = pool.tile([P, PARITIES, PASSES, P], U8, align_bytes=64)
+    for par in range(PARITIES):
+        for g0 in range(0, PASSES, 2):
+            flipped = banks.tile([P, 2, 2, P], F32, tag="bank")
+            for g in range(g0, g0 + 2):
+                for u in range(2):
+                    nc.tensor.transpose(
+                        flipped[:, g - g0, u, :],
+                        x_words[:, par, words_a_pass * g + u : words_a_pass * (g + 1) : 2],
+                        identity[:],
+                    )
+            copy = nc.vector.tensor_copy if g0 == 0 else nc.scalar.copy
+            copy(out=grouped_words[:, par, g0 : g0 + 2], in_=flipped[:].rearrange("p g u m -> p g m u"))
+        nc.vector.quantize_mx(
+            out=codes[:, par].rearrange("p g m -> p (g m)").bitcast(FP8X4),
+            scales=scales[:, par].rearrange("p g m -> p (g m)"),
+            in_=grouped[:, par].rearrange("p g m j -> p (g m j)"),
+        )
+    return codes, scales
+
+
+def rotate(nc, scratch, result, cos, sin, neg_sin):
+    rotated = result[:, :, :, 0:ROTARY]
+    pairs = rotated.rearrange("p h par (i two) -> p h par i two", two=2)
+    by_pair = [P, HEADS, PARITIES, PAIRS]
+    cross = scratch.tile([P, 2, HEADS, PARITIES, PAIRS], F32)
+    nc.vector.tensor_tensor(
+        out=cross[:, 0], in0=pairs[:, :, :, :, 1], in1=neg_sin.unsqueeze(1).to_broadcast(by_pair), op=ALU.mult
+    )
+    nc.vector.tensor_tensor(
+        out=cross[:, 1], in0=pairs[:, :, :, :, 0], in1=sin.unsqueeze(1).to_broadcast(by_pair), op=ALU.mult
+    )
+    nc.vector.tensor_tensor(
+        out=rotated, in0=rotated, in1=cos.unsqueeze(1).to_broadcast([P, HEADS, PARITIES, ROTARY]), op=ALU.mult
+    )
+    nc.vector.tensor_tensor(
+        out=pairs, in0=pairs, in1=cross[:].rearrange("p two h par i -> p h par i two"), op=ALU.add
+    )
+
+
+def tile_ttcodegenattention_pa_kernel(
+    tc, hidden_states, w_qkv_words, w_qkv_scales, out_0, out_1, out_2
+):
+    nc = tc.nc
+    blocks = ((0, out_0, True), (2, out_1, True), (1, out_2, False))
+    with tc.tile_pool(name="resident", bufs=1) as resident:
+        with tc.tile_pool(name="results", bufs=SHARDS * len(blocks)) as results:
+            with tc.tile_pool(name="scratch", bufs=2) as scratch:
+                with tc.psum_pool(name="banks", bufs=8) as banks:
+                    x_sb = load_tokens(nc, resident, hidden_states)
+                    shards = [load_shard(nc, resident, w_qkv_words, w_qkv_scales, s) for s in range(SHARDS)]
+                    cos, sin, neg_sin = rotary_tables(nc, resident)
+                    x_codes, x_scales = quantise_tokens(nc, resident, banks, x_sb)
+
+                    for s in range(SHARDS):
+                        w_words, w_scales = shards[s]
+                        for block, out, is_rotated in blocks:
+                            result = results.tile([P, HEADS, PARITIES, HEAD_DIM], F32)
+                            for par in range(PARITIES):
+                                acc = banks.tile([P, BLOCK], F32, tag="bank")
+                                for g in range(PASSES):
+                                    nc.tensor.matmul_mx(
+                                        out=acc[:],
+                                        lhsT=x_codes[:, par, g, :].bitcast(FP8X4),
+                                        lhsT_scale=x_scales[:, par, g, :],
+                                        rhs=w_words[:, g, 2 * BLOCK * block : 2 * BLOCK * (block + 1)].bitcast(FP4X4),
+                                        rhs_scale=w_scales[:, g, BLOCK * block : BLOCK * (block + 1)],
+                                        start=(g == 0),
+                                        stop=(g == PASSES - 1),
+                                    )
+                                nc.scalar.copy(
+                                    out=result[:, :, par, :], in_=acc[:].rearrange("p (h c) -> p h c", h=HEADS)
+                                )
+                            if is_rotated:
+                                rotate(nc, scratch, result, cos, sin, neg_sin)
+                            for b in range(BATCH):
+                                nc.sync.dma_start(
+                                    out=out[b, HEADS * s : HEADS * (s + 1)].rearrange(
+                                        "h (pair par) c -> pair h (par c)", par=PARITIES
+                                    ),
+                                    in_=result[b:P:BATCH].rearrange("p h par c -> p h (par c)"),
+                                )

@@ -45,28 +45,38 @@ def load_tokens(nc, pool, hidden_states):
     return x_sb
 
 
-def load_shard(nc, pool, w_qkv_words, w_qkv_scales, s):
-    scales = pool.tile([P, PASSES, SHARD_COLS], U8, name="w_scales%d" % s, align_bytes=64)
-    scales_i32 = scales[:].bitcast(I32)
-    nc.vector.memset(scales_i32, 0)
-    cols = slice(s * SHARD_COLS // 4, (s + 1) * SHARD_COLS // 4)
+def scale_partition(q):
+    return 32 * (q // 4) + q % 4
+
+
+def load_scales(nc, pool, w_qkv_scales, first_shard, n_shards):
+    width = n_shards * SHARD_COLS
+    scales = pool.tile([P, PASSES, width], U8, name="w_scales%d" % first_shard, align_bytes=64)
+    nc.vector.memset(scales[:].bitcast(I32), 0)
+    cols = slice(first_shard * SHARD_COLS // 4, (first_shard + n_shards) * SHARD_COLS // 4)
     for q in range(SCALE_ROWS // 2):
         nc.sync.dma_start(
-            out=scales_i32[32 * (q // 4) + q % 4 : P : 64],
+            out=scales[:].bitcast(I32)[scale_partition(q) : P : 64],
             in_=w_qkv_scales.bitcast(I32)[:, q : SCALE_ROWS : SCALE_ROWS // 2, cols].rearrange("g q n -> q g n"),
         )
-    words = pool.tile([P, PASSES, 2 * SHARD_COLS], U8, name="w_words%d" % s, align_bytes=64)
-    cols = slice(s * SHARD_COLS // 2, (s + 1) * SHARD_COLS // 2)
-    nc.sync.dma_start(
-        out=words[:].bitcast(I32),
-        in_=w_qkv_words.bitcast(I32)[:, :, cols].rearrange("g p n -> p g n"),
-    )
-    return words, scales
+    return scales
 
 
-def rotary_tables(nc, pool):
-    partition = pool.tile([P, 1], I32)
-    nc.gpsimd.iota(partition[:], pattern=[[0, 1]], base=0, channel_multiplier=1)
+def load_words(nc, pool, w_qkv_words, s, pieces):
+    views = {}
+    for first, count in pieces:
+        part = pool.tile([P, PASSES, 2 * BLOCK * count], U8, name="w_words%d_%d" % (s, first), align_bytes=64)
+        start = (s * SHARD_COLS + first * BLOCK) // 2
+        nc.sync.dma_start(
+            out=part[:].bitcast(I32),
+            in_=w_qkv_words.bitcast(I32)[:, :, start : start + count * BLOCK // 2].rearrange("g p n -> p g n"),
+        )
+        for i in range(count):
+            views[first + i] = part[:, :, 2 * BLOCK * i : 2 * BLOCK * (i + 1)]
+    return views
+
+
+def rotary_tables(nc, pool, partition):
     position = pool.tile([P, PARITIES], I32)
     for par in range(PARITIES):
         nc.vector.tensor_scalar(
@@ -118,9 +128,7 @@ def rotary_tables(nc, pool):
     return cos, sin, neg_sin
 
 
-def quantise_tokens(nc, pool, banks, x_sb):
-    identity = pool.tile([P, P], F32)
-    make_identity(nc, identity[:])
+def quantise_tokens(nc, pool, banks, x_sb, identity):
     x_words = x_sb[:].bitcast(F32)
     words_a_pass = P * PACK // 2
     grouped = pool.tile([P, PARITIES, PASSES, P, PACK], BF16, align_bytes=64)
@@ -176,12 +184,23 @@ def tile_ttcodegenattention_pa_kernel(
             with tc.tile_pool(name="scratch", bufs=2) as scratch:
                 with tc.psum_pool(name="banks", bufs=8) as banks:
                     x_sb = load_tokens(nc, resident, hidden_states)
-                    shards = [load_shard(nc, resident, w_qkv_words, w_qkv_scales, s) for s in range(SHARDS)]
-                    cos, sin, neg_sin = rotary_tables(nc, resident)
-                    x_codes, x_scales = quantise_tokens(nc, resident, banks, x_sb)
+                    identity = resident.tile([P, P], F32)
+                    make_identity(nc, identity[:])
+                    partition = resident.tile([P, 1], I32)
+                    nc.gpsimd.iota(partition[:], pattern=[[0, 1]], base=0, channel_multiplier=1)
+                    scales = [load_scales(nc, resident, w_qkv_scales, 0, 2)]
+                    words = [load_words(nc, resident, w_qkv_words, 0, ((0, 1), (1, 2)))]
+                    words.append(load_words(nc, resident, w_qkv_words, 1, ((0, 3),)))
+                    scales.append(load_scales(nc, resident, w_qkv_scales, 2, 2))
+                    words.append(load_words(nc, resident, w_qkv_words, 2, ((0, 3),)))
+                    words.append(load_words(nc, resident, w_qkv_words, 3, ((0, 3),)))
+                    cos, sin, neg_sin = rotary_tables(nc, resident, partition)
+                    x_codes, x_scales = quantise_tokens(nc, resident, banks, x_sb, identity)
 
                     for s in range(SHARDS):
-                        w_words, w_scales = shards[s]
+                        w_words = words[s]
+                        w_scales = scales[s // 2]
+                        scale_base = (s % 2) * SHARD_COLS
                         for block, out, is_rotated in blocks:
                             result = results.tile([P, HEADS, PARITIES, HEAD_DIM], F32)
                             for par in range(PARITIES):
@@ -191,8 +210,8 @@ def tile_ttcodegenattention_pa_kernel(
                                         out=acc[:],
                                         lhsT=x_codes[:, par, g, :].bitcast(FP8X4),
                                         lhsT_scale=x_scales[:, par, g, :],
-                                        rhs=w_words[:, g, 2 * BLOCK * block : 2 * BLOCK * (block + 1)].bitcast(FP4X4),
-                                        rhs_scale=w_scales[:, g, BLOCK * block : BLOCK * (block + 1)],
+                                        rhs=w_words[block][:, g, :].bitcast(FP4X4),
+                                        rhs_scale=w_scales[:, g, scale_base + BLOCK * block : scale_base + BLOCK * (block + 1)],
                                         start=(g == 0),
                                         stop=(g == PASSES - 1),
                                     )

@@ -131,27 +131,34 @@ def rotary_tables(nc, pool, partition):
 def quantise_tokens(nc, pool, banks, x_sb, identity):
     x_words = x_sb[:].bitcast(F32)
     words_a_pass = P * PACK // 2
-    grouped = pool.tile([P, PARITIES, PASSES, P, PACK], BF16, align_bytes=64)
-    grouped_words = grouped[:].bitcast(F32)
-    codes = pool.tile([P, PARITIES, PASSES, P], U32, align_bytes=64)
-    scales = pool.tile([P, PARITIES, PASSES, P], U8, align_bytes=64)
+    flipped = {}
     for par in range(PARITIES):
         for g0 in range(0, PASSES, 2):
-            flipped = banks.tile([P, 2, 2, P], F32, tag="bank")
+            bank = banks.tile([P, 2, 2, P], F32, tag="bank")
             for g in range(g0, g0 + 2):
                 for u in range(2):
                     nc.tensor.transpose(
-                        flipped[:, g - g0, u, :],
+                        bank[:, g - g0, u, :],
                         x_words[:, par, words_a_pass * g + u : words_a_pass * (g + 1) : 2],
                         identity[:],
                     )
-            copy = nc.vector.tensor_copy if g0 == 0 else nc.scalar.copy
-            copy(out=grouped_words[:, par, g0 : g0 + 2], in_=flipped[:].rearrange("p g u m -> p g m u"))
+            flipped[(par, g0)] = bank
+    codes = []
+    scales = []
+    for par in range(PARITIES):
+        grouped = pool.tile([P, PASSES, P, PACK], BF16, name="grouped%d" % par, align_bytes=64)
+        grouped_words = grouped[:].bitcast(F32)
+        nc.vector.tensor_copy(out=grouped_words[:, 0:2], in_=flipped[(par, 0)][:].rearrange("p g u m -> p g m u"))
+        nc.scalar.copy(out=grouped_words[:, 2:4], in_=flipped[(par, 2)][:].rearrange("p g u m -> p g m u"))
+        code = pool.tile([P, PASSES, P], U32, name="x_codes%d" % par, align_bytes=64)
+        scale = pool.tile([P, PASSES, P], U8, name="x_scales%d" % par, align_bytes=64)
         nc.vector.quantize_mx(
-            out=codes[:, par].rearrange("p g m -> p (g m)").bitcast(FP8X4),
-            scales=scales[:, par].rearrange("p g m -> p (g m)"),
-            in_=grouped[:, par].rearrange("p g m j -> p (g m j)"),
+            out=code[:].rearrange("p g m -> p (g m)").bitcast(FP8X4),
+            scales=scale[:].rearrange("p g m -> p (g m)"),
+            in_=grouped[:].rearrange("p g m j -> p (g m j)"),
         )
+        codes.append(code)
+        scales.append(scale)
     return codes, scales
 
 
@@ -178,52 +185,56 @@ def tile_ttcodegenattention_pa_kernel(
     tc, hidden_states, w_qkv_words, w_qkv_scales, out_0, out_1, out_2
 ):
     nc = tc.nc
-    blocks = ((0, out_0, True), (2, out_1, True), (1, out_2, False))
+    queries, values, keys = (0, out_0, True), (1, out_2, False), (2, out_1, True)
+    order = []
+    for s in range(SHARDS - 2):
+        order.extend([(s, queries), (s, keys), (s, values)])
+    for s in range(SHARDS - 2, SHARDS):
+        order.extend([(s, queries), (s, keys)])
+    for s in range(SHARDS - 2, SHARDS):
+        order.append((s, values))
     with tc.tile_pool(name="resident", bufs=1) as resident:
-        with tc.tile_pool(name="results", bufs=SHARDS * len(blocks)) as results:
+        with tc.tile_pool(name="results", bufs=len(order)) as results:
             with tc.tile_pool(name="scratch", bufs=2) as scratch:
-                with tc.psum_pool(name="banks", bufs=8) as banks:
+                with tc.psum_pool(name="banks", bufs=8) as banks, tc.manual_schedule():
                     x_sb = load_tokens(nc, resident, hidden_states)
                     identity = resident.tile([P, P], F32)
                     make_identity(nc, identity[:])
                     partition = resident.tile([P, 1], I32)
                     nc.gpsimd.iota(partition[:], pattern=[[0, 1]], base=0, channel_multiplier=1)
-                    scales = [load_scales(nc, resident, w_qkv_scales, 0, 2)]
+                    scales = [load_scales(nc, resident, w_qkv_scales, 0, 1)]
                     words = [load_words(nc, resident, w_qkv_words, 0, ((0, 1), (1, 2)))]
+                    scales.append(load_scales(nc, resident, w_qkv_scales, 1, 1))
                     words.append(load_words(nc, resident, w_qkv_words, 1, ((0, 3),)))
-                    scales.append(load_scales(nc, resident, w_qkv_scales, 2, 2))
-                    words.append(load_words(nc, resident, w_qkv_words, 2, ((0, 3),)))
-                    words.append(load_words(nc, resident, w_qkv_words, 3, ((0, 3),)))
                     cos, sin, neg_sin = rotary_tables(nc, resident, partition)
                     x_codes, x_scales = quantise_tokens(nc, resident, banks, x_sb, identity)
+                    for s in range(2, SHARDS):
+                        scales.append(load_scales(nc, resident, w_qkv_scales, s, 1))
+                        words.append(load_words(nc, resident, w_qkv_words, s, ((0, 3),)))
 
-                    for s in range(SHARDS):
-                        w_words = words[s]
-                        w_scales = scales[s // 2]
-                        scale_base = (s % 2) * SHARD_COLS
-                        for block, out, is_rotated in blocks:
-                            result = results.tile([P, HEADS, PARITIES, HEAD_DIM], F32)
-                            for par in range(PARITIES):
-                                acc = banks.tile([P, BLOCK], F32, tag="bank")
-                                for g in range(PASSES):
-                                    nc.tensor.matmul_mx(
-                                        out=acc[:],
-                                        lhsT=x_codes[:, par, g, :].bitcast(FP8X4),
-                                        lhsT_scale=x_scales[:, par, g, :],
-                                        rhs=w_words[block][:, g, :].bitcast(FP4X4),
-                                        rhs_scale=w_scales[:, g, scale_base + BLOCK * block : scale_base + BLOCK * (block + 1)],
-                                        start=(g == 0),
-                                        stop=(g == PASSES - 1),
-                                    )
-                                nc.scalar.copy(
-                                    out=result[:, :, par, :], in_=acc[:].rearrange("p (h c) -> p h c", h=HEADS)
+                    for s, (block, out, is_rotated) in order:
+                        result = results.tile([P, HEADS, PARITIES, HEAD_DIM], F32)
+                        for par in range(PARITIES):
+                            acc = banks.tile([P, BLOCK], F32, tag="bank")
+                            for g in range(PASSES):
+                                nc.tensor.matmul_mx(
+                                    out=acc[:],
+                                    lhsT=x_codes[par][:, g, :].bitcast(FP8X4),
+                                    lhsT_scale=x_scales[par][:, g, :],
+                                    rhs=words[s][block][:, g, :].bitcast(FP4X4),
+                                    rhs_scale=scales[s][:, g, BLOCK * block : BLOCK * (block + 1)],
+                                    start=(g == 0),
+                                    stop=(g == PASSES - 1),
                                 )
-                            if is_rotated:
-                                rotate(nc, scratch, result, cos, sin, neg_sin)
-                            for b in range(BATCH):
-                                nc.sync.dma_start(
-                                    out=out[b, HEADS * s : HEADS * (s + 1)].rearrange(
-                                        "h (pair par) c -> pair h (par c)", par=PARITIES
-                                    ),
-                                    in_=result[b:P:BATCH].rearrange("p h par c -> p h (par c)"),
-                                )
+                            nc.scalar.copy(
+                                out=result[:, :, par, :], in_=acc[:].rearrange("p (h c) -> p h c", h=HEADS)
+                            )
+                        if is_rotated:
+                            rotate(nc, scratch, result, cos, sin, neg_sin)
+                        for b in range(BATCH):
+                            nc.sync.dma_start(
+                                out=out[b, HEADS * s : HEADS * (s + 1)].rearrange(
+                                    "h (pair par) c -> pair h (par c)", par=PARITIES
+                                ),
+                                in_=result[b:P:BATCH].rearrange("p h par c -> p h (par c)"),
+                            )

@@ -49,16 +49,22 @@ def scale_partition(q):
     return 32 * (q // 4) + q % 4
 
 
-def load_scales(nc, pool, w_qkv_scales, first_shard, n_shards):
+def load_scales(nc, pool, w_qkv_scales, first_shard, n_shards, on_gpsimd):
     width = n_shards * SHARD_COLS
     scales = pool.tile([P, PASSES, width], U8, name="w_scales%d" % first_shard, align_bytes=64)
     nc.vector.memset(scales[:].bitcast(I32), 0)
     cols = slice(first_shard * SHARD_COLS // 4, (first_shard + n_shards) * SHARD_COLS // 4)
     for q in range(SCALE_ROWS // 2):
-        nc.sync.dma_start(
-            out=scales[:].bitcast(I32)[scale_partition(q) : P : 64],
-            in_=w_qkv_scales.bitcast(I32)[:, q : SCALE_ROWS : SCALE_ROWS // 2, cols].rearrange("g q n -> q g n"),
-        )
+        if on_gpsimd:
+            nc.gpsimd.dma_start(
+                out=scales[:].bitcast(F32)[scale_partition(q) : P : 64],
+                in_=w_qkv_scales.bitcast(F32)[:, q : SCALE_ROWS : SCALE_ROWS // 2, cols].rearrange("g q n -> q g n"),
+            )
+        else:
+            nc.sync.dma_start(
+                out=scales[:].bitcast(I32)[scale_partition(q) : P : 64],
+                in_=w_qkv_scales.bitcast(I32)[:, q : SCALE_ROWS : SCALE_ROWS // 2, cols].rearrange("g q n -> q g n"),
+            )
     return scales
 
 
@@ -202,18 +208,20 @@ def tile_ttcodegenattention_pa_kernel(
                     make_identity(nc, identity[:])
                     partition = resident.tile([P, 1], I32)
                     nc.gpsimd.iota(partition[:], pattern=[[0, 1]], base=0, channel_multiplier=1)
-                    scales = [load_scales(nc, resident, w_qkv_scales, 0, 1)]
+                    late_scales = load_scales(nc, resident, w_qkv_scales, 2, 2, True)
+                    scales = [load_scales(nc, resident, w_qkv_scales, 0, 1, False)]
                     words = [load_words(nc, resident, w_qkv_words, 0, ((0, 1), (1, 2)))]
-                    scales.append(load_scales(nc, resident, w_qkv_scales, 1, 1))
+                    scales.append(load_scales(nc, resident, w_qkv_scales, 1, 1, False))
                     words.append(load_words(nc, resident, w_qkv_words, 1, ((0, 3),)))
+                    for s in range(2, SHARDS):
+                        scales.append(late_scales)
+                        words.append(load_words(nc, resident, w_qkv_words, s, ((0, 3),)))
                     cos, sin, neg_sin = rotary_tables(nc, resident, partition)
                     x_codes, x_scales = quantise_tokens(nc, resident, banks, x_sb, identity)
-                    for s in range(2, SHARDS):
-                        scales.append(load_scales(nc, resident, w_qkv_scales, s, 1))
-                        words.append(load_words(nc, resident, w_qkv_words, s, ((0, 3),)))
 
                     for s, (block, out, is_rotated) in order:
                         result = results.tile([P, HEADS, PARITIES, HEAD_DIM], F32)
+                        scale_base = (s - 2) * SHARD_COLS if s >= 2 else 0
                         for par in range(PARITIES):
                             acc = banks.tile([P, BLOCK], F32, tag="bank")
                             for g in range(PASSES):
@@ -222,7 +230,7 @@ def tile_ttcodegenattention_pa_kernel(
                                     lhsT=x_codes[par][:, g, :].bitcast(FP8X4),
                                     lhsT_scale=x_scales[par][:, g, :],
                                     rhs=words[s][block][:, g, :].bitcast(FP4X4),
-                                    rhs_scale=scales[s][:, g, BLOCK * block : BLOCK * (block + 1)],
+                                    rhs_scale=scales[s][:, g, scale_base + BLOCK * block : scale_base + BLOCK * (block + 1)],
                                     start=(g == 0),
                                     stop=(g == PASSES - 1),
                                 )

@@ -54,17 +54,18 @@ def load_scales(nc, pool, w_qkv_scales, first_shard, n_shards, on_gpsimd):
     scales = pool.tile([P, PASSES, width], U8, name="w_scales%d" % first_shard, align_bytes=64)
     nc.vector.memset(scales[:].bitcast(I32), 0)
     cols = slice(first_shard * SHARD_COLS // 4, (first_shard + n_shards) * SHARD_COLS // 4)
-    for q in range(SCALE_ROWS // 2):
-        if on_gpsimd:
+    if on_gpsimd:
+        for r in range(4):
             nc.gpsimd.dma_start(
-                out=scales[:].bitcast(F32)[scale_partition(q) : P : 64],
-                in_=w_qkv_scales.bitcast(F32)[:, q : SCALE_ROWS : SCALE_ROWS // 2, cols].rearrange("g q n -> q g n"),
+                out=scales[:].bitcast(F32)[r:P:32],
+                in_=w_qkv_scales.bitcast(F32)[:, r:SCALE_ROWS:4, cols].rearrange("g q n -> q g n"),
             )
-        else:
-            nc.sync.dma_start(
-                out=scales[:].bitcast(I32)[scale_partition(q) : P : 64],
-                in_=w_qkv_scales.bitcast(I32)[:, q : SCALE_ROWS : SCALE_ROWS // 2, cols].rearrange("g q n -> q g n"),
-            )
+        return scales
+    for q in range(SCALE_ROWS // 2):
+        nc.sync.dma_start(
+            out=scales[:].bitcast(I32)[scale_partition(q) : P : 64],
+            in_=w_qkv_scales.bitcast(I32)[:, q : SCALE_ROWS : SCALE_ROWS // 2, cols].rearrange("g q n -> q g n"),
+        )
     return scales
 
 
@@ -193,12 +194,8 @@ def tile_ttcodegenattention_pa_kernel(
     nc = tc.nc
     queries, values, keys = (0, out_0, True), (1, out_2, False), (2, out_1, True)
     order = []
-    for s in range(SHARDS - 2):
+    for s in range(SHARDS):
         order.extend([(s, queries), (s, keys), (s, values)])
-    for s in range(SHARDS - 2, SHARDS):
-        order.extend([(s, queries), (s, keys)])
-    for s in range(SHARDS - 2, SHARDS):
-        order.append((s, values))
     with tc.tile_pool(name="resident", bufs=1) as resident:
         with tc.tile_pool(name="results", bufs=len(order)) as results:
             with tc.tile_pool(name="scratch", bufs=2) as scratch:
@@ -208,20 +205,19 @@ def tile_ttcodegenattention_pa_kernel(
                     make_identity(nc, identity[:])
                     partition = resident.tile([P, 1], I32)
                     nc.gpsimd.iota(partition[:], pattern=[[0, 1]], base=0, channel_multiplier=1)
-                    late_scales = load_scales(nc, resident, w_qkv_scales, 2, 2, True)
                     scales = [load_scales(nc, resident, w_qkv_scales, 0, 1, False)]
                     words = [load_words(nc, resident, w_qkv_words, 0, ((0, 1), (1, 2)))]
                     scales.append(load_scales(nc, resident, w_qkv_scales, 1, 1, False))
                     words.append(load_words(nc, resident, w_qkv_words, 1, ((0, 3),)))
-                    for s in range(2, SHARDS):
-                        scales.append(late_scales)
-                        words.append(load_words(nc, resident, w_qkv_words, s, ((0, 3),)))
                     cos, sin, neg_sin = rotary_tables(nc, resident, partition)
                     x_codes, x_scales = quantise_tokens(nc, resident, banks, x_sb, identity)
+                    scales.append(load_scales(nc, resident, w_qkv_scales, 2, 1, False))
+                    for s in range(2, SHARDS):
+                        words.append(load_words(nc, resident, w_qkv_words, s, ((0, 3),)))
+                    scales.append(load_scales(nc, resident, w_qkv_scales, 3, 1, True))
 
                     for s, (block, out, is_rotated) in order:
                         result = results.tile([P, HEADS, PARITIES, HEAD_DIM], F32)
-                        scale_base = (s - 2) * SHARD_COLS if s >= 2 else 0
                         for par in range(PARITIES):
                             acc = banks.tile([P, BLOCK], F32, tag="bank")
                             for g in range(PASSES):
@@ -230,7 +226,7 @@ def tile_ttcodegenattention_pa_kernel(
                                     lhsT=x_codes[par][:, g, :].bitcast(FP8X4),
                                     lhsT_scale=x_scales[par][:, g, :],
                                     rhs=words[s][block][:, g, :].bitcast(FP4X4),
-                                    rhs_scale=scales[s][:, g, scale_base + BLOCK * block : scale_base + BLOCK * (block + 1)],
+                                    rhs_scale=scales[s][:, g, BLOCK * block : BLOCK * (block + 1)],
                                     start=(g == 0),
                                     stop=(g == PASSES - 1),
                                 )

import math

import concourse.mybir as mybir
from concourse.masks import make_identity

F32 = mybir.dt.float32
BF16 = mybir.dt.bfloat16
I32 = mybir.dt.int32
U32 = mybir.dt.uint32
U8 = mybir.dt.uint8
FP8X4 = mybir.dt.float8_e4m3fn_x4
FP4X4 = mybir.dt.float4_e2m1fn_x4
ALU = mybir.AluOpType
ACT = mybir.ActivationFunctionType

P = 128
BATCH = 2
CHANNELS = 2048
PACK = 4
PASSES = CHANNELS // (P * PACK)
PARITIES = 2

SHARDS = 4
HEADS = 4
HEAD_DIM = 128
BLOCK = HEADS * HEAD_DIM
SHARD_COLS = 3 * BLOCK
SCALE_ROWS = 16

ROTARY = 64
PAIRS = ROTARY // 2
ROPE_BASE = 10000.0
ROUND_MAGIC = 1.5 * 2.0**23

FLOPS = 2 * BATCH * 128 * CHANNELS * SHARDS * SHARD_COLS


def load_tokens(nc, pool, hidden_states):
    x_sb = pool.tile([P, PARITIES, CHANNELS], BF16)
    for b in range(BATCH):
        nc.sync.dma_start(
            out=x_sb[b:P:BATCH],
            in_=hidden_states[b].rearrange("(pair par) e -> pair par e", par=PARITIES),
        )
    return x_sb


def scale_partition(q):
    return 32 * (q // 4) + q % 4


def load_scales(nc, pool, w_qkv_scales, first_shard, n_shards, on_gpsimd):
    width = n_shards * SHARD_COLS
    scales = pool.tile([P, PASSES, width], U8, name="w_scales%d" % first_shard, align_bytes=64)
    nc.vector.memset(scales[:].bitcast(I32), 0)
    cols = slice(first_shard * SHARD_COLS // 4, (first_shard + n_shards) * SHARD_COLS // 4)
    if on_gpsimd:
        for r in range(4):
            nc.gpsimd.dma_start(
                out=scales[:].bitcast(F32)[r:P:32],
                in_=w_qkv_scales.bitcast(F32)[:, r:SCALE_ROWS:4, cols].rearrange("g q n -> q g n"),
            )
        return scales
    for q in range(SCALE_ROWS // 2):
        nc.sync.dma_start(
            out=scales[:].bitcast(I32)[scale_partition(q) : P : 64],
            in_=w_qkv_scales.bitcast(I32)[:, q : SCALE_ROWS : SCALE_ROWS // 2, cols].rearrange("g q n -> q g n"),
        )
    return scales


def load_words(nc, pool, w_qkv_words, s, pieces):
    views = {}
    for first, count in pieces:
        part = pool.tile([P, PASSES, 2 * BLOCK * count], U8, name="w_words%d_%d" % (s, first), align_bytes=64)
        start = (s * SHARD_COLS + first * BLOCK) // 2
        nc.sync.dma_start(
            out=part[:].bitcast(I32),
            in_=w_qkv_words.bitcast(I32)[:, :, start : start + count * BLOCK // 2].rearrange("g p n -> p g n"),
        )
        for i in range(count):
            views[first + i] = part[:, :, 2 * BLOCK * i : 2 * BLOCK * (i + 1)]
    return views


def rotary_tables(nc, pool, partition):
    position = pool.tile([P, PARITIES], I32)
    for par in range(PARITIES):
        nc.vector.tensor_scalar(
            out=position[:, par : par + 1],
            in0=partition[:],
            scalar1=P - 2,
            scalar2=par,
            op0=ALU.bitwise_and,
            op1=ALU.bitwise_or,
        )
    phase = pool.tile([P, 3 * ROTARY], F32)
    turns = phase[:, 0:ROTARY].rearrange("p (par i) -> p par i", par=PARITIES)
    nc.vector.tensor_scalar(
        out=turns[:, :, 0:1],
        in0=position[:].unsqueeze(2),
        scalar1=1.0 / (2.0 * math.pi),
        scalar2=None,
        op0=ALU.mult,
    )
    n = 1
    while n < PAIRS:
        nc.vector.tensor_scalar(
            out=turns[:, :, n : 2 * n],
            in0=turns[:, :, 0:n],
            scalar1=ROPE_BASE ** (-2.0 * n / ROTARY),
            scalar2=None,
            op0=ALU.mult,
        )
        n *= 2
    nc.vector.tensor_scalar(
        out=phase[:, ROTARY : 3 * ROTARY].rearrange("p (par i two) -> p par i two", par=PARITIES, two=2),
        in0=turns.unsqueeze(3).to_broadcast([P, PARITIES, PAIRS, 2]),
        scalar1=0.25,
        scalar2=None,
        op0=ALU.add,
    )
    whole = pool.tile([P, 3 * ROTARY], F32)
    nc.vector.tensor_scalar(
        out=whole[:], in0=phase[:], scalar1=ROUND_MAGIC, scalar2=ROUND_MAGIC, op0=ALU.add, op1=ALU.subtract
    )
    nc.vector.tensor_tensor(out=phase[:], in0=phase[:], in1=whole[:], op=ALU.subtract)
    trig = pool.tile([P, 3 * ROTARY], F32)
    nc.scalar.activation(out=trig[:], in_=phase[:], func=ACT.Sin, scale=2.0 * math.pi)
    minus = pool.tile([P, ROTARY], F32)
    nc.scalar.activation(out=minus[:], in_=phase[:, 0:ROTARY], func=ACT.Sin, scale=-2.0 * math.pi)
    cos = trig[:, ROTARY : 3 * ROTARY].rearrange("p (par c) -> p par c", par=PARITIES)
    sin = trig[:, 0:ROTARY].rearrange("p (par i) -> p par i", par=PARITIES)
    neg_sin = minus[:].rearrange("p (par i) -> p par i", par=PARITIES)
    return cos, sin, neg_sin


def quantise_tokens(nc, pool, banks, x_sb, identity):
    x_words = x_sb[:].bitcast(F32)
    words_a_pass = P * PACK // 2
    flipped = {}
    for par in range(PARITIES):
        for g0 in range(0, PASSES, 2):
            bank = banks.tile([P, 2, 2, P], F32, tag="bank")
            for g in range(g0, g0 + 2):
                for u in range(2):
                    nc.tensor.transpose(
                        bank[:, g - g0, u, :],
                        x_words[:, par, words_a_pass * g + u : words_a_pass * (g + 1) : 2],
                        identity[:],
                    )
            flipped[(par, g0)] = bank
    codes = []
    scales = []
    for par in range(PARITIES):
        grouped = pool.tile([P, PASSES, P, PACK], BF16, name="grouped%d" % par, align_bytes=64)
        grouped_words = grouped[:].bitcast(F32)
        nc.vector.tensor_copy(out=grouped_words[:, 0:2], in_=flipped[(par, 0)][:].rearrange("p g u m -> p g m u"))
        nc.scalar.copy(out=grouped_words[:, 2:4], in_=flipped[(par, 2)][:].rearrange("p g u m -> p g m u"))
        code = pool.tile([P, PASSES, P], U32, name="x_codes%d" % par, align_bytes=64)
        scale = pool.tile([P, PASSES, P], U8, name="x_scales%d" % par, align_bytes=64)
        nc.vector.quantize_mx(
            out=code[:].rearrange("p g m -> p (g m)").bitcast(FP8X4),
            scales=scale[:].rearrange("p g m -> p (g m)"),
            in_=grouped[:].rearrange("p g m j -> p (g m j)"),
        )
        codes.append(code)
        scales.append(scale)
    return codes, scales


def rotate(nc, scratch, result, cos, sin, neg_sin):
    rotated = result[:, :, :, 0:ROTARY]
    pairs = rotated.rearrange("p h par (i two) -> p h par i two", two=2)
    by_pair = [P, HEADS, PARITIES, PAIRS]
    cross = scratch.tile([P, 2, HEADS, PARITIES, PAIRS], F32)
    nc.vector.tensor_tensor(
        out=cross[:, 0], in0=pairs[:, :, :, :, 1], in1=neg_sin.unsqueeze(1).to_broadcast(by_pair), op=ALU.mult
    )
    nc.vector.tensor_tensor(
        out=cross[:, 1], in0=pairs[:, :, :, :, 0], in1=sin.unsqueeze(1).to_broadcast(by_pair), op=ALU.mult
    )
    nc.vector.tensor_tensor(
        out=rotated, in0=rotated, in1=cos.unsqueeze(1).to_broadcast([P, HEADS, PARITIES, ROTARY]), op=ALU.mult
    )
    nc.vector.tensor_tensor(
        out=pairs, in0=pairs, in1=cross[:].rearrange("p two h par i -> p h par i two"), op=ALU.add
    )


def tile_ttcodegenattention_pa_kernel(
    tc, hidden_states, w_qkv_words, w_qkv_scales, out_0, out_1, out_2
):
    nc = tc.nc
    queries, values, keys = (0, out_0, True), (1, out_2, False), (2, out_1, True)
    order = []
    for s in range(SHARDS):
        order.extend([(s, queries), (s, keys), (s, values)])
    with tc.tile_pool(name="resident", bufs=1) as resident:
        with tc.tile_pool(name="results", bufs=len(order)) as results:
            with tc.tile_pool(name="scratch", bufs=2) as scratch:
                with tc.psum_pool(name="banks", bufs=8) as banks, tc.manual_schedule():
                    x_sb = load_tokens(nc, resident, hidden_states)
                    identity = resident.tile([P, P], F32)
                    make_identity(nc, identity[:])
                    partition = resident.tile([P, 1], I32)
                    nc.gpsimd.iota(partition[:], pattern=[[0, 1]], base=0, channel_multiplier=1)
                    scales = [load_scales(nc, resident, w_qkv_scales, 0, 1, False)]
                    words = [load_words(nc, resident, w_qkv_words, 0, ((0, 1), (1, 2)))]
                    scales.append(load_scales(nc, resident, w_qkv_scales, 1, 1, False))
                    words.append(load_words(nc, resident, w_qkv_words, 1, ((0, 3),)))
                    cos, sin, neg_sin = rotary_tables(nc, resident, partition)
                    x_codes, x_scales = quantise_tokens(nc, resident, banks, x_sb, identity)
                    scales.append(load_scales(nc, resident, w_qkv_scales, 2, 1, False))
                    for s in range(2, SHARDS):
                        words.append(load_words(nc, resident, w_qkv_words, s, ((0, 3),)))
                    scales.append(load_scales(nc, resident, w_qkv_scales, 3, 1, True))

                    for s, (block, out, is_rotated) in order:
                        result = results.tile([P, HEADS, PARITIES, HEAD_DIM], F32)
                        for par in range(PARITIES):
                            acc = banks.tile([P, BLOCK], F32, tag="bank")
                            for g in range(PASSES):
                                nc.tensor.matmul_mx(
                                    out=acc[:],
                                    lhsT=x_codes[par][:, g, :].bitcast(FP8X4),
                                    lhsT_scale=x_scales[par][:, g, :],
                                    rhs=words[s][block][:, g, :].bitcast(FP4X4),
                                    rhs_scale=scales[s][:, g, BLOCK * block : BLOCK * (block + 1)],
                                    start=(g == 0),
                                    stop=(g == PASSES - 1),
                                )
                            nc.scalar.copy(
                                out=result[:, :, par, :], in_=acc[:].rearrange("p (h c) -> p h c", h=HEADS)
                            )
                        if is_rotated:
                            rotate(nc, scratch, result, cos, sin, neg_sin)
                        for b in range(BATCH):
                            nc.sync.dma_start(
                                out=out[b, HEADS * s : HEADS * (s + 1)].rearrange(
                                    "h (pair par) c -> pair h (par c)", par=PARITIES
                                ),
                                in_=result[b:P:BATCH].rearrange("p h par c -> p h (par c)"),
                            )
